import numpy as np
import ml_dtypes


def mxq(x, axis, fmt="e4m3"):
    dtype, down = {"e4m3": (ml_dtypes.float8_e4m3fn, 7), "e5m2": (ml_dtypes.float8_e5m2, 14)}[fmt]
    v = np.moveaxis(np.asarray(x, np.float32).astype(ml_dtypes.bfloat16).astype(np.float64), axis, -1)
    blocks = v.reshape(v.shape[:-1] + (-1, 32))
    amax = np.abs(blocks).max(-1, keepdims=True)
    byte = np.maximum(np.where(amax > 0, np.frexp(amax)[1] - 1 + 127, 0) - down, 1)
    scale = np.exp2(byte - 127.0)
    codes = (blocks / scale).astype(np.float32).astype(dtype).astype(np.float64)
    return np.moveaxis((codes * scale).reshape(v.shape), -1, axis)


WIDE = False


def mx_kscale(k):
    if not WIDE:
        return np.ones(k)
    levels = np.array([10, -10, 5, -5, 0])
    a = np.random.permutation(np.resize(levels, k // 512 * 4)).reshape(k // 512, 4)
    idx = np.arange(k)
    return np.exp2(a[idx // 512, idx % 128 // 32])


BF16 = ml_dtypes.bfloat16


def bf(x):
    return np.asarray(x, np.float32).astype(BF16)


def f64(x):
    return np.asarray(x).astype(np.float64)


E2M1 = np.array([0.0, 0.5, 1.0, 1.5, 2.0, 3.0, 4.0, 6.0, -0.0, -0.5, -1.0, -1.5, -2.0, -3.0, -4.0, -6.0])


def pack_weight(w, fmt):
    k, n = w.shape
    w = f64(bf(w)).reshape(k // 32, 32, n)
    amax = np.abs(w).max(1)
    if fmt == "e4m3":
        byte = np.frexp(amax)[1] - 1 + 127 - 7
    else:
        mant, ex = np.frexp(amax / 6.0)
        byte = np.where(mant > 0.5, ex, ex - 1) + 127
    byte = np.clip(np.where(amax > 0, byte, 1), 1, 254)
    scaled = (w * np.exp2(127.0 - byte)[:, None, :]).reshape(k, n).astype(np.float32)
    by_word = np.ascontiguousarray(scaled.reshape(k // 512, 128, 4, n).transpose(0, 1, 3, 2))
    if fmt == "e4m3":
        words = by_word.astype(ml_dtypes.float8_e4m3fn).view(np.uint8)
    else:
        c = by_word.astype(ml_dtypes.float4_e2m1fn).view(np.uint8) & 0xF
        words = c[..., 0::2] | (c[..., 1::2] << 4)
    return np.ascontiguousarray(words), np.ascontiguousarray(byte.astype(np.uint8).reshape(k // 512, 16, n))


def unpack_weight(words, scales, fmt):
    g, p, n, _ = words.shape
    if fmt == "e4m3":
        vals = np.ascontiguousarray(words).view(ml_dtypes.float8_e4m3fn).astype(np.float64)
    else:
        nib = np.empty((g, p, n, 4), np.uint8)
        nib[..., 0::2] = words & 0xF
        nib[..., 1::2] = words >> 4
        vals = E2M1[nib]
    vals = vals * np.repeat(np.exp2(scales.astype(np.float64) - 127.0), 8, axis=1)[..., None]
    return vals.transpose(0, 1, 3, 2).reshape(g * 512, n)


B, A, E, H, NEXP, NACT = 512, 8, 512, 512, 4, 128
M = B * A
FMT = "e4m3"


def sigmoid(v):
    return 1.0 / (1.0 + np.exp(-v))


def setup_inputs():
    s, t = mx_kscale(H), mx_kscale(H)
    h = bf(np.random.standard_normal((M, H)) * 0.65 * s)
    gate_logit = bf(np.random.standard_normal((M, NEXP)))
    w1 = np.random.standard_normal((NEXP, H, H)) * 1.5 / np.sqrt(H) / s[None, None, :] * t[None, :, None]
    e_b1 = bf(np.random.standard_normal((NEXP, H)) * 0.3 * t[None, :])
    w2 = np.random.standard_normal((NEXP, NACT, H)) * 2.0 / np.sqrt(H) / t[None, None, :]
    e_b2 = bf(np.random.standard_normal((NEXP, NACT)) * 0.3)
    w1_words, w1_scales = pack_weight(np.ascontiguousarray(np.swapaxes(w1, 1, 2)).reshape(-1, H), FMT)
    w2_words, w2_scales = pack_weight(np.ascontiguousarray(np.swapaxes(w2, 1, 2)).reshape(-1, NACT), FMT)
    return {
        "h": h,
        "gate_logit": gate_logit,
        "e_w1_words": w1_words,
        "e_w1_scales": w1_scales,
        "e_b1": e_b1,
        "e_w2_words": w2_words,
        "e_w2_scales": w2_scales,
        "e_b2": e_b2,
    }


def reference(h, gate_logit, e_w1_words, e_w1_scales, e_b1, e_w2_words, e_w2_scales, e_b2):
    hq = mxq(f64(h), 1, "e4m3")
    h1 = np.maximum((hq @ unpack_weight(e_w1_words, e_w1_scales, FMT).reshape(NEXP, H, H)) + f64(e_b1)[:, None, :], 0.0)
    experts_out = (mxq(h1, 2, "e4m3") @ unpack_weight(e_w2_words, e_w2_scales, FMT).reshape(NEXP, H, NACT)) + f64(e_b2)[:, None, :]
    weight = sigmoid(f64(gate_logit))
    w = weight.T[:, :, None]
    final_q = (experts_out * w).mean(axis=0)
    return final_q, np.swapaxes(experts_out, 0, 1)

@@ -1,0 +1,252 @@
+from contextlib import ExitStack
+
+import concourse.mybir as mybir
+from concourse.masks import make_identity
+
+F32 = mybir.dt.float32
+BF16 = mybir.dt.bfloat16
+U8 = mybir.dt.uint8
+U32 = mybir.dt.uint32
+I32 = mybir.dt.int32
+FP8X4 = mybir.dt.float8_e4m3fn_x4
+ADD = mybir.AluOpType.add
+MULT = mybir.AluOpType.mult
+ACT = mybir.ActivationFunctionType
+
+P = 128
+ROWS = 4096
+HID = 512
+NEXP = 4
+NACT = 128
+TILES = ROWS // P
+PAIR = 2
+LOAD = 4
+PLANES = 2
+
+FLOPS = 2 * ROWS * HID * HID * NEXP + 2 * ROWS * HID * NACT * NEXP
+
+
+def tile_mspagent_pb_t_e_kernel(
+    tc, h, gate_logit, e_w1_words, e_w1_scales, e_b1, e_w2_words, e_w2_scales, e_b2, out_0, out_1
+):
+    nc = tc.nc
+    with ExitStack() as ctx:
+        keep = ctx.enter_context(tc.tile_pool(name="keep", bufs=1))
+        work = ctx.enter_context(tc.tile_pool(name="work", bufs=2))
+        outs = ctx.enter_context(tc.tile_pool(name="outs", bufs=3))
+        psum_x = ctx.enter_context(tc.psum_pool(name="psum_x", bufs=1))
+        psum_t = ctx.enter_context(tc.psum_pool(name="psum_t", bufs=2))
+        psum_y = ctx.enter_context(tc.psum_pool(name="psum_y", bufs=1))
+        ctx.enter_context(tc.manual_schedule())
+
+        h_rows = h.rearrange("(p i) k -> p i k", i=TILES)
+        out_q = out_0.rearrange("(p i) a -> p i a", i=TILES)
+        out_y = out_1.rearrange("(p i) e a -> p i (e a)", i=TILES)
+
+        h_sb = keep.tile([P, TILES, HID], BF16)
+        w1_words = keep.tile([P, NEXP, 4 * HID], U8, align_bytes=64)
+        w2_words = keep.tile([P, NEXP, 4 * NACT], U8, align_bytes=64)
+        w1_scales = keep.tile([P, HID], U8, align_bytes=64)
+        w2_scales = keep.tile([P, NACT], U8, align_bytes=64)
+        nc.vector.memset(w1_scales[:].bitcast(I32), 0)
+        nc.vector.memset(w2_scales[:].bitcast(I32), 0)
+
+        nc.sync.dma_start(out=h_sb[:, 0:LOAD, :], in_=h_rows[:, 0:LOAD, :])
+        for quadrant in range(4):
+            nc.sync.dma_start(
+                out=w1_scales[32 * quadrant : 32 * quadrant + 16, :].bitcast(I32),
+                in_=e_w1_scales[:, 4 * quadrant : 4 * quadrant + 4, :].bitcast(I32),
+            )
+        nc.sync.dma_start(
+            out=w1_words[:].bitcast(I32),
+            in_=e_w1_words.rearrange("g p n t -> p g (n t)").bitcast(I32),
+        )
+        for quadrant in range(4):
+            nc.sync.dma_start(
+                out=w2_scales[32 * quadrant : 32 * quadrant + 16, :].bitcast(I32),
+                in_=e_w2_scales[:, 4 * quadrant : 4 * quadrant + 4, :].bitcast(I32),
+            )
+        nc.sync.dma_start(
+            out=w2_words[:].bitcast(I32),
+            in_=e_w2_words.rearrange("g p n t -> p g (n t)").bitcast(I32),
+        )
+        for first in range(LOAD, TILES, LOAD):
+            nc.sync.dma_start(out=h_sb[:, first : first + LOAD, :], in_=h_rows[:, first : first + LOAD, :])
+
+        b1_all = keep.tile([P, NEXP, HID], BF16)
+        b2_all = keep.tile([P, NEXP * NACT], BF16)
+        logits = keep.tile([P, TILES * NEXP], BF16)
+        nc.scalar.dma_start(out=logits[:], in_=gate_logit.rearrange("(p i) e -> p (i e)", i=TILES))
+        nc.scalar.dma_start(
+            out=b1_all[:].rearrange("p e n -> p (e n)"),
+            in_=e_b1.rearrange("e n -> (e n)").partition_broadcast(P),
+        )
+        nc.scalar.dma_start(out=b2_all[:], in_=e_b2.rearrange("e a -> (e a)").partition_broadcast(P))
+
+        identity = keep.tile([P, P], F32)
+        make_identity(nc, identity[:])
+
+        sigmoids = keep.tile([P, TILES * NEXP], F32)
+        gates = keep.tile([P, TILES, NEXP], F32)
+        nc.scalar.activation(out=sigmoids[:], in_=logits[:], func=ACT.Sigmoid)
+        nc.gpsimd.tensor_scalar_mul(out=gates[:].rearrange("p i e -> p (i e)"), in0=sigmoids[:], scalar1=0.25)
+
+        h_codes = keep.tile([P, TILES, P], U32, align_bytes=64)
+        h_scales = keep.tile([P, TILES * P], U8, align_bytes=64)
+
+        ht_banks, h_grouped = {}, {}
+        x_banks, z_tiles, zt_banks, h1_grouped, h1_codes, h1_scales, y_banks, y_tiles = {}, {}, {}, {}, {}, {}, {}, {}
+
+        def transpose_h(pair):
+            ht = psum_y.tile([P, PLANES, PAIR, P], F32, tag="ht")
+            for j in range(PAIR):
+                words = h_sb[:, PAIR * pair + j, :].bitcast(F32)
+                for u in range(PLANES):
+                    nc.tensor.transpose(ht[:, u, j, :], words[:, u : HID // 2 : PLANES], identity[:])
+            ht_banks[pair] = ht
+
+        def regroup_h(pair):
+            grouped = work.tile([P, PAIR, P, 4], BF16, tag="h_grouped", align_bytes=64)
+            nc.scalar.copy(
+                out=grouped[:].rearrange("p j m t -> p (j m t)").bitcast(F32).rearrange("p (q u) -> p q u", u=PLANES),
+                in_=ht_banks[pair][:].rearrange("p u j m -> p (j m) u"),
+            )
+            h_grouped[pair] = grouped
+
+        def quantise_h(pair):
+            first = PAIR * pair
+            nc.vector.quantize_mx(
+                out=h_codes[:, first : first + PAIR, :].rearrange("p j m -> p (j m)").bitcast(FP8X4),
+                scales=h_scales[:, first * P : (first + PAIR) * P],
+                in_=h_grouped[pair][:].rearrange("p j m t -> p (j m t)"),
+            )
+
+        def first_matmul(i, e):
+            x = psum_x.tile([P, HID], F32, tag="x%d" % e)
+            nc.tensor.matmul_mx(
+                out=x[:],
+                lhsT=h_codes[:, i, :].bitcast(FP8X4),
+                lhsT_scale=h_scales[:, i * P : (i + 1) * P],
+                rhs=w1_words[:, e, :].bitcast(FP8X4),
+                rhs_scale=w1_scales[4 * e : P, :],
+                start=True,
+                stop=True,
+            )
+            x_banks[i, e] = x
+
+        def add_bias(i, e):
+            if e == 0:
+                z_new = work.tile([P, NEXP, PLANES, 2 * P], BF16, tag="z")
+                z_tiles[i] = z_new
+            nc.vector.tensor_tensor(
+                out=z_tiles[i][:, e].rearrange("m u (p c) -> m u p c", c=2),
+                in0=x_banks[i, e][:].rearrange("m (p u c) -> m u p c", u=PLANES, c=2),
+                in1=b1_all[:, e, :].rearrange("m (p u c) -> m u p c", u=PLANES, c=2),
+                op=ADD,
+            )
+
+        def transpose_z(i):
+            z = z_tiles[i]
+            for half in range(NEXP // PAIR):
+                zt = psum_t.tile([P, PLANES, PAIR, P], F32, tag="zt")
+                for j in range(PAIR):
+                    for u in range(PLANES):
+                        nc.tensor.transpose(zt[:, u, j, :], z[:, PAIR * half + j, u, :].bitcast(F32), identity[:])
+                zt_banks[i, half] = zt
+
+        def relu_and_regroup(i):
+            grouped = work.tile([P, NEXP, P, 4], BF16, tag="h1_grouped", align_bytes=64)
+            for half in range(NEXP // PAIR):
+                zt = zt_banks[i, half]
+                nc.scalar.activation(
+                    out=grouped[:, PAIR * half : PAIR * (half + 1)].rearrange("p j m (u c) -> p (j m) u c", u=PLANES),
+                    in_=zt[:].rearrange("p u j m -> p (u j m)").bitcast(BF16).rearrange("p (u q c) -> p q u c", u=PLANES, c=2),
+                    func=ACT.Relu,
+                )
+            h1_grouped[i] = grouped
+
+        def quantise_h1(i):
+            codes = work.tile([P, NEXP * P], U32, tag="h1_codes", align_bytes=64)
+            scales = work.tile([P, NEXP * P], U8, tag="h1_scales", align_bytes=64)
+            nc.vector.quantize_mx(
+                out=codes[:].bitcast(FP8X4),
+                scales=scales[:],
+                in_=h1_grouped[i][:].rearrange("p e m t -> p (e m t)"),
+            )
+            h1_codes[i], h1_scales[i] = codes, scales
+
+        def second_matmul(i):
+            y = psum_y.tile([P, NEXP, NACT], F32, tag="y")
+            codes, scales = h1_codes[i], h1_scales[i]
+            for e in range(NEXP):
+                nc.tensor.matmul_mx(
+                    out=y[:, e, :],
+                    lhsT=codes[:, e * P : (e + 1) * P].bitcast(FP8X4),
+                    lhsT_scale=scales[:, e * P : (e + 1) * P],
+                    rhs=w2_words[:, e, :].bitcast(FP8X4),
+                    rhs_scale=w2_scales[4 * e : P, :],
+                    start=True,
+                    stop=True,
+                )
+            y_banks[i] = y
+
+        def add_bias_2(i):
+            if i % PAIR == 0:
+                y_new = outs.tile([P, PAIR, NEXP, NACT], F32, tag="y_sb")
+                y_tiles[i // PAIR] = y_new
+            nc.vector.tensor_tensor(
+                out=y_tiles[i // PAIR][:, i % PAIR].rearrange("p e a -> p (e a)"),
+                in0=y_banks[i][:].rearrange("p e a -> p (e a)"),
+                in1=b2_all[:],
+                op=ADD,
+            )
+
+        def gate_and_store(pair):
+            first = PAIR * pair
+            y_sb = y_tiles[pair]
+            nc.sync.dma_start(out=out_y[:, first : first + PAIR, :], in_=y_sb[:].rearrange("p s e a -> p s (e a)"))
+            gated = outs.tile([P, PAIR, NEXP, NACT], F32, tag="gated")
+            nc.gpsimd.tensor_tensor(
+                out=gated[:],
+                in0=y_sb[:],
+                in1=gates[:, first : first + PAIR, :].unsqueeze(3).to_broadcast([P, PAIR, NEXP, NACT]),
+                op=MULT,
+            )
+            halves = outs.tile([P, PAIR, 2, NACT], F32, tag="halves")
+            nc.gpsimd.tensor_tensor(out=halves[:], in0=gated[:, :, 0:2, :], in1=gated[:, :, 2:4, :], op=ADD)
+            final_q = outs.tile([P, PAIR, NACT], F32, tag="final_q")
+            nc.gpsimd.tensor_tensor(out=final_q[:], in0=halves[:, :, 0, :], in1=halves[:, :, 1, :], op=ADD)
+            nc.sync.dma_start(out=out_q[:, first : first + PAIR, :], in_=final_q[:])
+
+        for pair in range(2):
+            transpose_h(pair)
+            regroup_h(pair)
+            quantise_h(pair)
+        for e in range(NEXP):
+            first_matmul(0, e)
+
+        for r in range(TILES + 2):
+            if r >= 2:
+                second_matmul(r - 2)
+            for e in range(NEXP):
+                if r < TILES:
+                    add_bias(r, e)
+                if r + 1 < TILES:
+                    first_matmul(r + 1, e)
+                if e == NEXP // 2 - 1 and r >= 2:
+                    add_bias_2(r - 2)
+            if r < TILES:
+                transpose_z(r)
+            next_pair = (r + 3) // PAIR
+            if r % PAIR == 1 and next_pair < TILES // PAIR:
+                transpose_h(next_pair)
+            if r < TILES:
+                relu_and_regroup(r)
+            if r % PAIR == 1 and next_pair < TILES // PAIR:
+                regroup_h(next_pair)
+            if 1 <= r <= TILES:
+                quantise_h1(r - 1)
+            if r % PAIR == 0 and r >= 2 and (r + 2) // PAIR < TILES // PAIR:
+                quantise_h((r + 2) // PAIR)
+            if r >= 2 and (r - 2) % PAIR == PAIR - 1:
+                gate_and_store((r - 2) // PAIR)

@@ -57,10 +57,11 @@ def tile_mspagent_pb_t_e_kernel(
                 out=w1_scales[32 * quadrant : 32 * quadrant + 16, :].bitcast(I32),
                 in_=e_w1_scales[:, 4 * quadrant : 4 * quadrant + 4, :].bitcast(I32),
             )
-        nc.sync.dma_start(
-            out=w1_words[:].bitcast(I32),
-            in_=e_w1_words.rearrange("g p n t -> p g (n t)").bitcast(I32),
-        )
+        for e in range(NEXP):
+            nc.sync.dma_start(
+                out=w1_words[:, e, :].bitcast(I32),
+                in_=e_w1_words[e].rearrange("p n t -> p (n t)").bitcast(I32),
+            )
         for quadrant in range(4):
             nc.sync.dma_start(
                 out=w2_scales[32 * quadrant : 32 * quadrant + 16, :].bitcast(I32),
@@ -77,10 +78,8 @@ def tile_mspagent_pb_t_e_kernel(
         b2_all = keep.tile([P, NEXP * NACT], BF16)
         logits = keep.tile([P, TILES * NEXP], BF16)
         nc.scalar.dma_start(out=logits[:], in_=gate_logit.rearrange("(p i) e -> p (i e)", i=TILES))
-        nc.scalar.dma_start(
-            out=b1_all[:].rearrange("p e n -> p (e n)"),
-            in_=e_b1.rearrange("e n -> (e n)").partition_broadcast(P),
-        )
+        for e in range(NEXP):
+            nc.scalar.dma_start(out=b1_all[:, e, :], in_=e_b1[e].partition_broadcast(P))
         nc.scalar.dma_start(out=b2_all[:], in_=e_b2.rearrange("e a -> (e a)").partition_broadcast(P))
 
         identity = keep.tile([P, P], F32)
@@ -95,7 +94,7 @@ def tile_mspagent_pb_t_e_kernel(
         h_scales = keep.tile([P, TILES * P], U8, align_bytes=64)
 
         ht_banks, h_grouped = {}, {}
-        x_banks, z_tiles, zt_banks, h1_grouped, h1_codes, h1_scales, y_banks, y_tiles = {}, {}, {}, {}, {}, {}, {}, {}
+        x_banks, z_tiles, zt_banks, h1_grouped, h1_codes, h1_scales, y_banks, y_tiles, q_tiles = {}, {}, {}, {}, {}, {}, {}, {}, {}
 
         def transpose_h(pair):
             ht = psum_y.tile([P, PLANES, PAIR, P], F32, tag="ht")
@@ -201,22 +200,27 @@ def tile_mspagent_pb_t_e_kernel(
                 op=ADD,
             )
 
-        def gate_and_store(pair):
-            first = PAIR * pair
-            y_sb = y_tiles[pair]
-            nc.sync.dma_start(out=out_y[:, first : first + PAIR, :], in_=y_sb[:].rearrange("p s e a -> p s (e a)"))
-            gated = outs.tile([P, PAIR, NEXP, NACT], F32, tag="gated")
+        def gate(i):
+            if i % PAIR == 0:
+                q_new = outs.tile([P, PAIR, NACT], F32, tag="final_q")
+                q_tiles[i // PAIR] = q_new
+            gated = outs.tile([P, NEXP, NACT], F32, tag="gated")
             nc.gpsimd.tensor_tensor(
                 out=gated[:],
-                in0=y_sb[:],
-                in1=gates[:, first : first + PAIR, :].unsqueeze(3).to_broadcast([P, PAIR, NEXP, NACT]),
+                in0=y_tiles[i // PAIR][:, i % PAIR],
+                in1=gates[:, i, :].unsqueeze(2).to_broadcast([P, NEXP, NACT]),
                 op=MULT,
             )
-            halves = outs.tile([P, PAIR, 2, NACT], F32, tag="halves")
-            nc.gpsimd.tensor_tensor(out=halves[:], in0=gated[:, :, 0:2, :], in1=gated[:, :, 2:4, :], op=ADD)
-            final_q = outs.tile([P, PAIR, NACT], F32, tag="final_q")
-            nc.gpsimd.tensor_tensor(out=final_q[:], in0=halves[:, :, 0, :], in1=halves[:, :, 1, :], op=ADD)
-            nc.sync.dma_start(out=out_q[:, first : first + PAIR, :], in_=final_q[:])
+            halves = outs.tile([P, 2, NACT], F32, tag="halves")
+            nc.gpsimd.tensor_tensor(out=halves[:], in0=gated[:, 0:2, :], in1=gated[:, 2:4, :], op=ADD)
+            nc.gpsimd.tensor_tensor(out=q_tiles[i // PAIR][:, i % PAIR, :], in0=halves[:, 0, :], in1=halves[:, 1, :], op=ADD)
+
+        def store(pair):
+            first = PAIR * pair
+            nc.sync.dma_start(
+                out=out_y[:, first : first + PAIR, :], in_=y_tiles[pair][:].rearrange("p s e a -> p s (e a)")
+            )
+            nc.sync.dma_start(out=out_q[:, first : first + PAIR, :], in_=q_tiles[pair][:])
 
         for pair in range(2):
             transpose_h(pair)
@@ -225,28 +229,29 @@ def tile_mspagent_pb_t_e_kernel(
         for e in range(NEXP):
             first_matmul(0, e)
 
-        for r in range(TILES + 2):
-            if r >= 2:
-                second_matmul(r - 2)
+        for r in range(TILES + 3):
+            new_h = r % PAIR == 1 and r + 3 < TILES
+            if 1 <= r <= TILES:
+                transpose_z(r - 1)
+            if new_h:
+                transpose_h((r + 3) // PAIR)
+            if 3 <= r:
+                second_matmul(r - 3)
+            if 1 <= r <= TILES:
+                relu_and_regroup(r - 1)
+            if new_h:
+                regroup_h((r + 3) // PAIR)
             for e in range(NEXP):
                 if r < TILES:
                     add_bias(r, e)
                 if r + 1 < TILES:
                     first_matmul(r + 1, e)
-                if e == NEXP // 2 - 1 and r >= 2:
-                    add_bias_2(r - 2)
-            if r < TILES:
-                transpose_z(r)
-            next_pair = (r + 3) // PAIR
-            if r % PAIR == 1 and next_pair < TILES // PAIR:
-                transpose_h(next_pair)
-            if r < TILES:
-                relu_and_regroup(r)
-            if r % PAIR == 1 and next_pair < TILES // PAIR:
-                regroup_h(next_pair)
-            if 1 <= r <= TILES:
-                quantise_h1(r - 1)
-            if r % PAIR == 0 and r >= 2 and (r + 2) // PAIR < TILES // PAIR:
+            if 2 <= r <= TILES + 1:
+                quantise_h1(r - 2)
+            if r % PAIR == 0 and 2 <= r and r + 2 < TILES:
                 quantise_h((r + 2) // PAIR)
-            if r >= 2 and (r - 2) % PAIR == PAIR - 1:
-                gate_and_store((r - 2) // PAIR)
+            if 3 <= r:
+                add_bias_2(r - 3)
+                gate(r - 3)
+                if (r - 3) % PAIR == PAIR - 1:
+                    store((r - 3) // PAIR)

@@ -18,10 +18,15 @@ ROWS = 4096
 HID = 512
 NEXP = 4
 NACT = 128
+PACK = 4
 TILES = ROWS // P
+GROUP = 4
+GROUPS = TILES // GROUP
+WIDE = GROUP * P
+UNITS = GROUPS * NEXP
 PAIR = 2
-LOAD = 4
 PLANES = 2
+SCALAR_COLS = 128
 
 FLOPS = 2 * ROWS * HID * HID * NEXP + 2 * ROWS * HID * NACT * NEXP
 
@@ -32,55 +37,65 @@ def tile_mspagent_pb_t_e_kernel(
     nc = tc.nc
     with ExitStack() as ctx:
         keep = ctx.enter_context(tc.tile_pool(name="keep", bufs=1))
-        work = ctx.enter_context(tc.tile_pool(name="work", bufs=2))
+        work = ctx.enter_context(tc.tile_pool(name="work", bufs=3))
         outs = ctx.enter_context(tc.tile_pool(name="outs", bufs=3))
-        psum_x = ctx.enter_context(tc.psum_pool(name="psum_x", bufs=1))
-        psum_t = ctx.enter_context(tc.psum_pool(name="psum_t", bufs=2))
-        psum_y = ctx.enter_context(tc.psum_pool(name="psum_y", bufs=1))
+        psum_x = ctx.enter_context(tc.psum_pool(name="psum_x", bufs=4))
+        psum_y = ctx.enter_context(tc.psum_pool(name="psum_y", bufs=2))
+        psum_h = ctx.enter_context(tc.psum_pool(name="psum_h", bufs=2))
         ctx.enter_context(tc.manual_schedule())
 
         h_rows = h.rearrange("(p i) k -> p i k", i=TILES)
         out_q = out_0.rearrange("(p i) a -> p i a", i=TILES)
-        out_y = out_1.rearrange("(p i) e a -> p i (e a)", i=TILES)
+        out_y = out_1.rearrange("(p i) e a -> p i e a", i=TILES)
 
         h_sb = keep.tile([P, TILES, HID], BF16)
-        w1_words = keep.tile([P, NEXP, 4 * HID], U8, align_bytes=64)
-        w2_words = keep.tile([P, NEXP, 4 * NACT], U8, align_bytes=64)
+        w1_raw = keep.tile([P, NEXP, HID], I32, align_bytes=64)
+        w1_words = keep.tile([P, NEXP, HID], I32, align_bytes=64)
+        w2_words = keep.tile([P, NEXP, NACT], I32, align_bytes=64)
+        w1_scales_raw = keep.tile([P, HID], U8, align_bytes=64)
         w1_scales = keep.tile([P, HID], U8, align_bytes=64)
         w2_scales = keep.tile([P, NACT], U8, align_bytes=64)
-        nc.vector.memset(w1_scales[:].bitcast(I32), 0)
+        nc.vector.memset(w1_scales_raw[:].bitcast(I32), 0)
         nc.vector.memset(w2_scales[:].bitcast(I32), 0)
 
-        nc.sync.dma_start(out=h_sb[:, 0:LOAD, :], in_=h_rows[:, 0:LOAD, :])
+        for first in range(0, GROUP, PAIR):
+            nc.sync.dma_start(out=h_sb[:, first : first + PAIR, :], in_=h_rows[:, first : first + PAIR, :])
         for quadrant in range(4):
             nc.sync.dma_start(
-                out=w1_scales[32 * quadrant : 32 * quadrant + 16, :].bitcast(I32),
+                out=w1_scales_raw[32 * quadrant : 32 * quadrant + 16, :].bitcast(I32),
                 in_=e_w1_scales[:, 4 * quadrant : 4 * quadrant + 4, :].bitcast(I32),
             )
-        for e in range(NEXP):
-            nc.sync.dma_start(
-                out=w1_words[:, e, :].bitcast(I32),
-                in_=e_w1_words[e].rearrange("p n t -> p (n t)").bitcast(I32),
-            )
+        def load_w1(e):
+            nc.sync.dma_start(out=w1_raw[:, e, :], in_=e_w1_words[e].rearrange("p n t -> p (n t)").bitcast(I32))
+
+        def load_h(group):
+            first = group * GROUP
+            nc.sync.dma_start(out=h_sb[:, first : first + GROUP, :], in_=h_rows[:, first : first + GROUP, :])
+
+        load_w1(0)
+        load_w1(1)
+        load_h(1)
+        load_w1(2)
+        load_w1(3)
         for quadrant in range(4):
             nc.sync.dma_start(
                 out=w2_scales[32 * quadrant : 32 * quadrant + 16, :].bitcast(I32),
                 in_=e_w2_scales[:, 4 * quadrant : 4 * quadrant + 4, :].bitcast(I32),
             )
-        nc.sync.dma_start(
-            out=w2_words[:].bitcast(I32),
-            in_=e_w2_words.rearrange("g p n t -> p g (n t)").bitcast(I32),
-        )
-        for first in range(LOAD, TILES, LOAD):
-            nc.sync.dma_start(out=h_sb[:, first : first + LOAD, :], in_=h_rows[:, first : first + LOAD, :])
+        nc.sync.dma_start(out=w2_words[:], in_=e_w2_words.rearrange("g p n t -> p g (n t)").bitcast(I32))
+        for group in range(2, GROUPS):
+            load_h(group)
 
-        b1_all = keep.tile([P, NEXP, HID], BF16)
-        b2_all = keep.tile([P, NEXP * NACT], BF16)
         logits = keep.tile([P, TILES * NEXP], BF16)
+        b1_raw = keep.tile([P, NEXP, PACK], BF16)
+        b2_all = keep.tile([P, NEXP * NACT], BF16)
         nc.scalar.dma_start(out=logits[:], in_=gate_logit.rearrange("(p i) e -> p (i e)", i=TILES))
-        for e in range(NEXP):
-            nc.scalar.dma_start(out=b1_all[:, e, :], in_=e_b1[e].partition_broadcast(P))
+        nc.scalar.dma_start(out=b1_raw[:], in_=e_b1.rearrange("e (p t) -> p e t", t=PACK))
         nc.scalar.dma_start(out=b2_all[:], in_=e_b2.rearrange("e a -> (e a)").partition_broadcast(P))
+
+        warm = keep.tile([P, 2], F32)
+        nc.gpsimd.memset(warm[:], 0.0)
+        nc.scalar.activation(out=warm[:, 1:2], in_=warm[:, 0:1], func=ACT.Sigmoid)
 
         identity = keep.tile([P, P], F32)
         make_identity(nc, identity[:])
@@ -90,168 +105,181 @@ def tile_mspagent_pb_t_e_kernel(
         nc.scalar.activation(out=sigmoids[:], in_=logits[:], func=ACT.Sigmoid)
         nc.gpsimd.tensor_scalar_mul(out=gates[:].rearrange("p i e -> p (i e)"), in0=sigmoids[:], scalar1=0.25)
 
-        h_codes = keep.tile([P, TILES, P], U32, align_bytes=64)
+        h_codes = keep.tile([P, TILES * P], U32, align_bytes=64)
         h_scales = keep.tile([P, TILES * P], U8, align_bytes=64)
+        b1 = keep.tile([P, NEXP * PACK], F32)
+
+        def permute_w1_scales():
+            nc.vector.tensor_copy(
+                out=w1_scales[:].rearrange("p (t m) -> p m t", t=PACK),
+                in_=w1_scales_raw[:].rearrange("p (m t) -> p m t", t=PACK),
+            )
+
+        def permute_w1(e):
+            nc.vector.tensor_copy(
+                out=w1_words[:, e, :].rearrange("p (t m) -> p t m", t=PACK),
+                in_=w1_raw[:, e, :].rearrange("p (m t) -> p t m", t=PACK),
+            )
 
         ht_banks, h_grouped = {}, {}
-        x_banks, z_tiles, zt_banks, h1_grouped, h1_codes, h1_scales, y_banks, y_tiles, q_tiles = {}, {}, {}, {}, {}, {}, {}, {}, {}
+        x_banks, z_tiles, h1_grouped, h1_codes, h1_scales, y_banks, y_tiles, q_tiles = {}, {}, {}, {}, {}, {}, {}, {}
 
-        def transpose_h(pair):
-            ht = psum_y.tile([P, PLANES, PAIR, P], F32, tag="ht")
-            for j in range(PAIR):
-                words = h_sb[:, PAIR * pair + j, :].bitcast(F32)
-                for u in range(PLANES):
-                    nc.tensor.transpose(ht[:, u, j, :], words[:, u : HID // 2 : PLANES], identity[:])
-            ht_banks[pair] = ht
+        def transpose_h(group):
+            for half in range(GROUP // PAIR):
+                ht = psum_h.tile([P, PLANES, PAIR, P], F32, tag="ht")
+                for j in range(PAIR):
+                    words = h_sb[:, GROUP * group + PAIR * half + j, :].bitcast(F32)
+                    for u in range(PLANES):
+                        nc.tensor.transpose(ht[:, u, j, :], words[:, u : HID // 2 : PLANES], identity[:])
+                ht_banks[group, half] = ht
 
-        def regroup_h(pair):
-            grouped = work.tile([P, PAIR, P, 4], BF16, tag="h_grouped", align_bytes=64)
-            nc.scalar.copy(
-                out=grouped[:].rearrange("p j m t -> p (j m t)").bitcast(F32).rearrange("p (q u) -> p q u", u=PLANES),
-                in_=ht_banks[pair][:].rearrange("p u j m -> p (j m) u"),
-            )
-            h_grouped[pair] = grouped
+        def regroup_h(group):
+            grouped = work.tile([P, GROUP, P, PACK], BF16, tag="h_grouped", align_bytes=64)
+            for half in range(GROUP // PAIR):
+                nc.scalar.copy(
+                    out=grouped[:, PAIR * half : PAIR * (half + 1)]
+                    .rearrange("p j m t -> p (j m t)")
+                    .bitcast(F32)
+                    .rearrange("p (q u) -> p q u", u=PLANES),
+                    in_=ht_banks[group, half][:].rearrange("p u j m -> p (j m) u"),
+                )
+            h_grouped[group] = grouped
 
-        def quantise_h(pair):
-            first = PAIR * pair
+        def quantise_h(group):
             nc.vector.quantize_mx(
-                out=h_codes[:, first : first + PAIR, :].rearrange("p j m -> p (j m)").bitcast(FP8X4),
-                scales=h_scales[:, first * P : (first + PAIR) * P],
-                in_=h_grouped[pair][:].rearrange("p j m t -> p (j m t)"),
+                out=h_codes[:, group * WIDE : (group + 1) * WIDE].bitcast(FP8X4),
+                scales=h_scales[:, group * WIDE : (group + 1) * WIDE],
+                in_=h_grouped[group][:].rearrange("p j m t -> p (j m t)"),
             )
 
-        def first_matmul(i, e):
-            x = psum_x.tile([P, HID], F32, tag="x%d" % e)
+        def first_matmul(unit, t):
+            group, e = divmod(unit, NEXP)
+            x = psum_x.tile([P, WIDE], F32, tag="x")
             nc.tensor.matmul_mx(
                 out=x[:],
-                lhsT=h_codes[:, i, :].bitcast(FP8X4),
-                lhsT_scale=h_scales[:, i * P : (i + 1) * P],
-                rhs=w1_words[:, e, :].bitcast(FP8X4),
-                rhs_scale=w1_scales[4 * e : P, :],
+                lhsT=w1_words[:, e, t * P : (t + 1) * P].bitcast(FP8X4),
+                lhsT_scale=w1_scales[4 * e : P, t * P : (t + 1) * P],
+                rhs=h_codes[:, group * WIDE : (group + 1) * WIDE].bitcast(FP8X4),
+                rhs_scale=h_scales[:, group * WIDE : (group + 1) * WIDE],
                 start=True,
                 stop=True,
             )
-            x_banks[i, e] = x
+            x_banks[unit, t] = x
 
-        def add_bias(i, e):
-            if e == 0:
-                z_new = work.tile([P, NEXP, PLANES, 2 * P], BF16, tag="z")
-                z_tiles[i] = z_new
-            nc.vector.tensor_tensor(
-                out=z_tiles[i][:, e].rearrange("m u (p c) -> m u p c", c=2),
-                in0=x_banks[i, e][:].rearrange("m (p u c) -> m u p c", u=PLANES, c=2),
-                in1=b1_all[:, e, :].rearrange("m (p u c) -> m u p c", u=PLANES, c=2),
-                op=ADD,
+        def relu(unit, t):
+            e = unit % NEXP
+            if t == 0:
+                z_new = work.tile([P, PACK, WIDE], BF16, tag="z")
+                z_tiles[unit] = z_new
+            nc.scalar.activation(
+                out=z_tiles[unit][:, t, :],
+                in_=x_banks[unit, t][:],
+                func=ACT.Relu,
+                bias=b1[:, PACK * e + t : PACK * e + t + 1],
             )
 
-        def transpose_z(i):
-            z = z_tiles[i]
-            for half in range(NEXP // PAIR):
-                zt = psum_t.tile([P, PLANES, PAIR, P], F32, tag="zt")
-                for j in range(PAIR):
-                    for u in range(PLANES):
-                        nc.tensor.transpose(zt[:, u, j, :], z[:, PAIR * half + j, u, :].bitcast(F32), identity[:])
-                zt_banks[i, half] = zt
+        def interleave_vector(unit):
+            grouped = work.tile([P, WIDE, PACK], BF16, tag="h1_grouped", align_bytes=64)
+            h1_grouped[unit] = grouped
+            cut = WIDE - SCALAR_COLS
+            nc.vector.tensor_copy(out=grouped[:, 0:cut, :], in_=z_tiles[unit][:, :, 0:cut].rearrange("p t c -> p c t"))
 
-        def relu_and_regroup(i):
-            grouped = work.tile([P, NEXP, P, 4], BF16, tag="h1_grouped", align_bytes=64)
-            for half in range(NEXP // PAIR):
-                zt = zt_banks[i, half]
-                nc.scalar.activation(
-                    out=grouped[:, PAIR * half : PAIR * (half + 1)].rearrange("p j m (u c) -> p (j m) u c", u=PLANES),
-                    in_=zt[:].rearrange("p u j m -> p (u j m)").bitcast(BF16).rearrange("p (u q c) -> p q u c", u=PLANES, c=2),
-                    func=ACT.Relu,
-                )
-            h1_grouped[i] = grouped
+        def interleave_scalar(unit):
+            cut = WIDE - SCALAR_COLS
+            nc.scalar.copy(
+                out=h1_grouped[unit][:, cut:WIDE, :], in_=z_tiles[unit][:, :, cut:WIDE].rearrange("p t c -> p c t")
+            )
 
-        def quantise_h1(i):
-            codes = work.tile([P, NEXP * P], U32, tag="h1_codes", align_bytes=64)
-            scales = work.tile([P, NEXP * P], U8, tag="h1_scales", align_bytes=64)
+        def quantise_h1(unit):
+            codes = work.tile([P, WIDE], U32, tag="h1_codes", align_bytes=64)
+            scales = work.tile([P, WIDE], U8, tag="h1_scales", align_bytes=64)
             nc.vector.quantize_mx(
                 out=codes[:].bitcast(FP8X4),
                 scales=scales[:],
-                in_=h1_grouped[i][:].rearrange("p e m t -> p (e m t)"),
+                in_=h1_grouped[unit][:].rearrange("p c t -> p (c t)"),
             )
-            h1_codes[i], h1_scales[i] = codes, scales
+            h1_codes[unit], h1_scales[unit] = codes, scales
 
-        def second_matmul(i):
-            y = psum_y.tile([P, NEXP, NACT], F32, tag="y")
-            codes, scales = h1_codes[i], h1_scales[i]
-            for e in range(NEXP):
+        def second_matmul(unit):
+            e = unit % NEXP
+            y = psum_y.tile([P, GROUP, NACT], F32, tag="y")
+            codes, scales = h1_codes[unit], h1_scales[unit]
+            for j in range(GROUP):
                 nc.tensor.matmul_mx(
-                    out=y[:, e, :],
-                    lhsT=codes[:, e * P : (e + 1) * P].bitcast(FP8X4),
-                    lhsT_scale=scales[:, e * P : (e + 1) * P],
+                    out=y[:, j, :],
+                    lhsT=codes[:, j * P : (j + 1) * P].bitcast(FP8X4),
+                    lhsT_scale=scales[:, j * P : (j + 1) * P],
                     rhs=w2_words[:, e, :].bitcast(FP8X4),
                     rhs_scale=w2_scales[4 * e : P, :],
                     start=True,
                     stop=True,
                 )
-            y_banks[i] = y
+            y_banks[unit] = y
 
-        def add_bias_2(i):
-            if i % PAIR == 0:
-                y_new = outs.tile([P, PAIR, NEXP, NACT], F32, tag="y_sb")
-                y_tiles[i // PAIR] = y_new
+        def add_bias_2(unit):
+            group, e = divmod(unit, NEXP)
+            if e == 0:
+                y_new = outs.tile([P, GROUP, NEXP, NACT], F32, tag="y_sb")
+                y_tiles[group] = y_new
             nc.vector.tensor_tensor(
-                out=y_tiles[i // PAIR][:, i % PAIR].rearrange("p e a -> p (e a)"),
-                in0=y_banks[i][:].rearrange("p e a -> p (e a)"),
-                in1=b2_all[:],
+                out=y_tiles[group][:, :, e, :],
+                in0=y_banks[unit][:],
+                in1=b2_all[:, e * NACT : (e + 1) * NACT].unsqueeze(1).to_broadcast([P, GROUP, NACT]),
                 op=ADD,
             )
-
-        def gate(i):
-            if i % PAIR == 0:
-                q_new = outs.tile([P, PAIR, NACT], F32, tag="final_q")
-                q_tiles[i // PAIR] = q_new
-            gated = outs.tile([P, NEXP, NACT], F32, tag="gated")
-            nc.gpsimd.tensor_tensor(
-                out=gated[:],
-                in0=y_tiles[i // PAIR][:, i % PAIR],
-                in1=gates[:, i, :].unsqueeze(2).to_broadcast([P, NEXP, NACT]),
-                op=MULT,
-            )
-            halves = outs.tile([P, 2, NACT], F32, tag="halves")
-            nc.gpsimd.tensor_tensor(out=halves[:], in0=gated[:, 0:2, :], in1=gated[:, 2:4, :], op=ADD)
-            nc.gpsimd.tensor_tensor(out=q_tiles[i // PAIR][:, i % PAIR, :], in0=halves[:, 0, :], in1=halves[:, 1, :], op=ADD)
-
-        def store(pair):
-            first = PAIR * pair
             nc.sync.dma_start(
-                out=out_y[:, first : first + PAIR, :], in_=y_tiles[pair][:].rearrange("p s e a -> p s (e a)")
+                out=out_y[:, group * GROUP : (group + 1) * GROUP, e, :], in_=y_tiles[group][:, :, e, :]
             )
-            nc.sync.dma_start(out=out_q[:, first : first + PAIR, :], in_=q_tiles[pair][:])
 
-        for pair in range(2):
-            transpose_h(pair)
-            regroup_h(pair)
-            quantise_h(pair)
-        for e in range(NEXP):
-            first_matmul(0, e)
+        def gate(unit):
+            group, e = divmod(unit, NEXP)
+            if e == 0:
+                q_new = outs.tile([P, GROUP, NACT], F32, tag="final_q")
+                q_tiles[group] = q_new
+            q = q_tiles[group]
+            for j in range(GROUP):
+                factor = gates[:, group * GROUP + j, e : e + 1]
+                if e == 0:
+                    nc.vector.tensor_scalar_mul(out=q[:, j, :], in0=y_tiles[group][:, j, e, :], scalar1=factor)
+                else:
+                    nc.vector.scalar_tensor_tensor(
+                        out=q[:, j, :], in0=y_tiles[group][:, j, e, :], scalar=factor, in1=q[:, j, :], op0=MULT, op1=ADD
+                    )
+            if e == NEXP - 1:
+                nc.sync.dma_start(out=out_q[:, group * GROUP : (group + 1) * GROUP, :], in_=q[:])
 
-        for r in range(TILES + 3):
-            new_h = r % PAIR == 1 and r + 3 < TILES
-            if 1 <= r <= TILES:
-                transpose_z(r - 1)
-            if new_h:
-                transpose_h((r + 3) // PAIR)
-            if 3 <= r:
-                second_matmul(r - 3)
-            if 1 <= r <= TILES:
-                relu_and_regroup(r - 1)
-            if new_h:
-                regroup_h((r + 3) // PAIR)
-            for e in range(NEXP):
-                if r < TILES:
-                    add_bias(r, e)
-                if r + 1 < TILES:
-                    first_matmul(r + 1, e)
-            if 2 <= r <= TILES + 1:
-                quantise_h1(r - 2)
-            if r % PAIR == 0 and 2 <= r and r + 2 < TILES:
-                quantise_h((r + 2) // PAIR)
-            if 3 <= r:
-                add_bias_2(r - 3)
-                gate(r - 3)
-                if (r - 3) % PAIR == PAIR - 1:
-                    store((r - 3) // PAIR)
+        transpose_h(0)
+        regroup_h(0)
+        permute_w1_scales()
+        permute_w1(0)
+        nc.vector.tensor_copy(out=b1[:], in_=b1_raw[:].rearrange("p e t -> p (e t)"))
+        quantise_h(0)
+        for t in range(PACK):
+            first_matmul(0, t)
+        for e in range(1, NEXP):
+            permute_w1(e)
+
+        for s in range(UNITS + 2):
+            group, e = divmod(s, NEXP)
+            for t in range(PACK):
+                if s < UNITS:
+                    relu(s, t)
+                if s + 1 < UNITS:
+                    first_matmul(s + 1, t)
+                if t == 0 and 1 <= s <= UNITS:
+                    interleave_vector(s - 1)
+                    interleave_scalar(s - 1)
+            if group + 1 < GROUPS:
+                if e == 0:
+                    transpose_h(group + 1)
+                if e == 1:
+                    regroup_h(group + 1)
+            if 2 <= s:
+                add_bias_2(s - 2)
+            if 1 <= s <= UNITS:
+                quantise_h1(s - 1)
+                second_matmul(s - 1)
+            if 2 <= s:
+                gate(s - 2)
+            if group + 1 < GROUPS and e == 2:
+                quantise_h(group + 1)

@@ -11,6 +11,7 @@ I32 = mybir.dt.int32
 FP8X4 = mybir.dt.float8_e4m3fn_x4
 ADD = mybir.AluOpType.add
 MULT = mybir.AluOpType.mult
+MAX = mybir.AluOpType.max
 ACT = mybir.ActivationFunctionType
 
 P = 128
@@ -26,7 +27,9 @@ WIDE = GROUP * P
 UNITS = GROUPS * NEXP
 PAIR = 2
 PLANES = 2
+RUN = 4
 SCALAR_COLS = 128
+VECTOR_BANKS = {0: 2, 1: 1}
 
 FLOPS = 2 * ROWS * HID * HID * NEXP + 2 * ROWS * HID * NACT * NEXP
 
@@ -171,23 +174,28 @@ def tile_mspagent_pb_t_e_kernel(
             if t == 0:
                 z_new = work.tile([P, PACK, WIDE], BF16, tag="z")
                 z_tiles[unit] = z_new
-            nc.scalar.activation(
-                out=z_tiles[unit][:, t, :],
-                in_=x_banks[unit, t][:],
-                func=ACT.Relu,
-                bias=b1[:, PACK * e + t : PACK * e + t + 1],
-            )
+            bias = b1[:, PACK * e + t : PACK * e + t + 1]
+            if t >= PACK - VECTOR_BANKS.get(unit, 0):
+                nc.vector.tensor_scalar(
+                    out=z_tiles[unit][:, t, :], in0=x_banks[unit, t][:], scalar1=bias, scalar2=0.0, op0=ADD, op1=MAX
+                )
+            else:
+                nc.scalar.activation(out=z_tiles[unit][:, t, :], in_=x_banks[unit, t][:], func=ACT.Relu, bias=bias)
 
         def interleave_vector(unit):
             grouped = work.tile([P, WIDE, PACK], BF16, tag="h1_grouped", align_bytes=64)
             h1_grouped[unit] = grouped
             cut = WIDE - SCALAR_COLS
-            nc.vector.tensor_copy(out=grouped[:, 0:cut, :], in_=z_tiles[unit][:, :, 0:cut].rearrange("p t c -> p c t"))
+            nc.vector.tensor_copy(
+                out=grouped[:, 0:cut, :].rearrange("p (c i) t -> p c t i", i=RUN),
+                in_=z_tiles[unit][:, :, 0:cut].rearrange("p t (c i) -> p c t i", i=RUN),
+            )
 
         def interleave_scalar(unit):
             cut = WIDE - SCALAR_COLS
             nc.scalar.copy(
-                out=h1_grouped[unit][:, cut:WIDE, :], in_=z_tiles[unit][:, :, cut:WIDE].rearrange("p t c -> p c t")
+                out=h1_grouped[unit][:, cut:WIDE, :].rearrange("p (c i) t -> p c t i", i=RUN),
+                in_=z_tiles[unit][:, :, cut:WIDE].rearrange("p t (c i) -> p c t i", i=RUN),
             )
 
         def quantise_h1(unit):
@@ -256,8 +264,7 @@ def tile_mspagent_pb_t_e_kernel(
         quantise_h(0)
         for t in range(PACK):
             first_matmul(0, t)
-        for e in range(1, NEXP):
-            permute_w1(e)
+        permute_w1(1)
 
         for s in range(UNITS + 2):
             group, e = divmod(s, NEXP)
@@ -269,6 +276,9 @@ def tile_mspagent_pb_t_e_kernel(
                 if t == 0 and 1 <= s <= UNITS:
                     interleave_vector(s - 1)
                     interleave_scalar(s - 1)
+            if s == 0:
+                permute_w1(2)
+                permute_w1(3)
             if group + 1 < GROUPS:
                 if e == 0:
                     transpose_h(group + 1)

@@ -28,7 +28,7 @@ UNITS = GROUPS * NEXP
 PAIR = 2
 PLANES = 2
 RUN = 4
-SCALAR_COLS = 128
+SCALAR_COLS = 96
 VECTOR_BANKS = {0: 2, 1: 1}
 
 FLOPS = 2 * ROWS * HID * HID * NEXP + 2 * ROWS * HID * NACT * NEXP

@@ -28,7 +28,7 @@ UNITS = GROUPS * NEXP
 PAIR = 2
 PLANES = 2
 RUN = 4
-SCALAR_COLS = 96
+SCALAR_COLS = 80
 VECTOR_BANKS = {0: 2, 1: 1}
 
 FLOPS = 2 * ROWS * HID * HID * NEXP + 2 * ROWS * HID * NACT * NEXP

@@ -27,7 +27,7 @@ WIDE = GROUP * P
 UNITS = GROUPS * NEXP
 PAIR = 2
 PLANES = 2
-RUN = 4
+RUN = 8
 SCALAR_COLS = 80
 VECTOR_BANKS = {0: 2, 1: 1}
 

@@ -28,7 +28,8 @@ UNITS = GROUPS * NEXP
 PAIR = 2
 PLANES = 2
 RUN = 8
-SCALAR_COLS = 80
+SCALAR_COLS = 64
+GPSIMD_COLS = 64
 VECTOR_BANKS = {0: 2, 1: 1}
 
 FLOPS = 2 * ROWS * HID * HID * NEXP + 2 * ROWS * HID * NACT * NEXP
@@ -40,7 +41,7 @@ def tile_mspagent_pb_t_e_kernel(
     nc = tc.nc
     with ExitStack() as ctx:
         keep = ctx.enter_context(tc.tile_pool(name="keep", bufs=1))
-        work = ctx.enter_context(tc.tile_pool(name="work", bufs=3))
+        work = ctx.enter_context(tc.tile_pool(name="work", bufs=4))
         outs = ctx.enter_context(tc.tile_pool(name="outs", bufs=3))
         psum_x = ctx.enter_context(tc.psum_pool(name="psum_x", bufs=4))
         psum_y = ctx.enter_context(tc.psum_pool(name="psum_y", bufs=2))
@@ -185,10 +186,21 @@ def tile_mspagent_pb_t_e_kernel(
         def interleave_vector(unit):
             grouped = work.tile([P, WIDE, PACK], BF16, tag="h1_grouped", align_bytes=64)
             h1_grouped[unit] = grouped
-            cut = WIDE - SCALAR_COLS
+            cut = WIDE - SCALAR_COLS - GPSIMD_COLS
             nc.vector.tensor_copy(
                 out=grouped[:, 0:cut, :].rearrange("p (c i) t -> p c t i", i=RUN),
                 in_=z_tiles[unit][:, :, 0:cut].rearrange("p t (c i) -> p c t i", i=RUN),
+            )
+
+        def interleave_gpsimd(unit):
+            rows = slice(WIDE - SCALAR_COLS - GPSIMD_COLS - RUN, WIDE - SCALAR_COLS)
+            nc.gpsimd.tensor_scalar(
+                out=h1_grouped[unit][:, rows, :],
+                in0=z_tiles[unit][:, :, rows].rearrange("p t c -> p c t"),
+                scalar1=1.0,
+                scalar2=0.0,
+                op0=MULT,
+                op1=ADD,
             )
 
         def interleave_scalar(unit):
@@ -266,16 +278,28 @@ def tile_mspagent_pb_t_e_kernel(
             first_matmul(0, t)
         permute_w1(1)
 
-        for s in range(UNITS + 2):
+        for s in range(UNITS + 4):
             group, e = divmod(s, NEXP)
+            if 1 <= s <= UNITS:
+                interleave_vector(s - 1)
+                interleave_gpsimd(s - 1)
+            if 2 <= s < UNITS + 2:
+                quantise_h1(s - 2)
+            if 3 <= s < UNITS + 3:
+                add_bias_2(s - 3)
+            if 4 <= s:
+                gate(s - 4)
+            if group + 1 < GROUPS and e == 2:
+                quantise_h(group + 1)
             for t in range(PACK):
                 if s < UNITS:
                     relu(s, t)
                 if s + 1 < UNITS:
                     first_matmul(s + 1, t)
                 if t == 0 and 1 <= s <= UNITS:
-                    interleave_vector(s - 1)
                     interleave_scalar(s - 1)
+                if t == 1 and 2 <= s < UNITS + 2:
+                    second_matmul(s - 2)
             if s == 0:
                 permute_w1(2)
                 permute_w1(3)
@@ -284,12 +308,3 @@ def tile_mspagent_pb_t_e_kernel(
                     transpose_h(group + 1)
                 if e == 1:
                     regroup_h(group + 1)
-            if 2 <= s:
-                add_bias_2(s - 2)
-            if 1 <= s <= UNITS:
-                quantise_h1(s - 1)
-                second_matmul(s - 1)
-            if 2 <= s:
-                gate(s - 2)
-            if group + 1 < GROUPS and e == 2:
-                quantise_h(group + 1)

@@ -28,7 +28,7 @@ UNITS = GROUPS * NEXP
 PAIR = 2
 PLANES = 2
 RUN = 8
-SCALAR_COLS = 64
+TENSOR_COLS = 64
 GPSIMD_COLS = 64
 VECTOR_BANKS = {0: 2, 1: 1}
 
@@ -44,7 +44,8 @@ def tile_mspagent_pb_t_e_kernel(
         work = ctx.enter_context(tc.tile_pool(name="work", bufs=4))
         outs = ctx.enter_context(tc.tile_pool(name="outs", bufs=3))
         psum_x = ctx.enter_context(tc.psum_pool(name="psum_x", bufs=4))
-        psum_y = ctx.enter_context(tc.psum_pool(name="psum_y", bufs=2))
+        psum_y = ctx.enter_context(tc.psum_pool(name="psum_y", bufs=1))
+        psum_z = ctx.enter_context(tc.psum_pool(name="psum_z", bufs=1))
         psum_h = ctx.enter_context(tc.psum_pool(name="psum_h", bufs=2))
         ctx.enter_context(tc.manual_schedule())
 
@@ -103,6 +104,8 @@ def tile_mspagent_pb_t_e_kernel(
 
         identity = keep.tile([P, P], F32)
         make_identity(nc, identity[:])
+        identity_bf16 = keep.tile([P, P], BF16)
+        make_identity(nc, identity_bf16[:])
 
         sigmoids = keep.tile([P, TILES * NEXP], F32)
         gates = keep.tile([P, TILES, NEXP], F32)
@@ -126,6 +129,7 @@ def tile_mspagent_pb_t_e_kernel(
             )
 
         ht_banks, h_grouped = {}, {}
+        zi_banks = {}
         x_banks, z_tiles, h1_grouped, h1_codes, h1_scales, y_banks, y_tiles, q_tiles = {}, {}, {}, {}, {}, {}, {}, {}
 
         def transpose_h(group):
@@ -186,14 +190,14 @@ def tile_mspagent_pb_t_e_kernel(
         def interleave_vector(unit):
             grouped = work.tile([P, WIDE, PACK], BF16, tag="h1_grouped", align_bytes=64)
             h1_grouped[unit] = grouped
-            cut = WIDE - SCALAR_COLS - GPSIMD_COLS
+            cut = WIDE - TENSOR_COLS - GPSIMD_COLS
             nc.vector.tensor_copy(
                 out=grouped[:, 0:cut, :].rearrange("p (c i) t -> p c t i", i=RUN),
                 in_=z_tiles[unit][:, :, 0:cut].rearrange("p t (c i) -> p c t i", i=RUN),
             )
 
         def interleave_gpsimd(unit):
-            rows = slice(WIDE - SCALAR_COLS - GPSIMD_COLS - RUN, WIDE - SCALAR_COLS)
+            rows = slice(WIDE - TENSOR_COLS - GPSIMD_COLS - RUN, WIDE - TENSOR_COLS)
             nc.gpsimd.tensor_scalar(
                 out=h1_grouped[unit][:, rows, :],
                 in0=z_tiles[unit][:, :, rows].rearrange("p t c -> p c t"),
@@ -203,11 +207,21 @@ def tile_mspagent_pb_t_e_kernel(
                 op1=ADD,
             )
 
-        def interleave_scalar(unit):
-            cut = WIDE - SCALAR_COLS
+        def interleave_tensor(unit):
+            zi = psum_z.tile([P, TENSOR_COLS, PACK], BF16, tag="zi")
+            nc.tensor.matmul(
+                out=zi[:].rearrange("p (c i) t -> p c t i", i=RUN),
+                lhsT=identity_bf16[:],
+                rhs=z_tiles[unit][:, :, WIDE - TENSOR_COLS : WIDE].rearrange("p t (c i) -> p c t i", i=RUN),
+                start=True,
+                stop=True,
+            )
+            zi_banks[unit] = zi
+
+        def fetch_interleaved(unit):
             nc.scalar.copy(
-                out=h1_grouped[unit][:, cut:WIDE, :].rearrange("p (c i) t -> p c t i", i=RUN),
-                in_=z_tiles[unit][:, :, cut:WIDE].rearrange("p t (c i) -> p c t i", i=RUN),
+                out=h1_grouped[unit][:, WIDE - TENSOR_COLS : WIDE, :].rearrange("p c t -> p (c t)"),
+                in_=zi_banks[unit][:].rearrange("p c t -> p (c t)"),
             )
 
         def quantise_h1(unit):
@@ -283,6 +297,7 @@ def tile_mspagent_pb_t_e_kernel(
             if 1 <= s <= UNITS:
                 interleave_vector(s - 1)
                 interleave_gpsimd(s - 1)
+                interleave_tensor(s - 1)
             if 2 <= s < UNITS + 2:
                 quantise_h1(s - 2)
             if 3 <= s < UNITS + 3:
@@ -296,9 +311,9 @@ def tile_mspagent_pb_t_e_kernel(
                     relu(s, t)
                 if s + 1 < UNITS:
                     first_matmul(s + 1, t)
-                if t == 0 and 1 <= s <= UNITS:
-                    interleave_scalar(s - 1)
-                if t == 1 and 2 <= s < UNITS + 2:
+                if t == PACK - 1 and 1 <= s <= UNITS:
+                    fetch_interleaved(s - 1)
+                if t == 2 and 2 <= s < UNITS + 2:
                     second_matmul(s - 2)
             if s == 0:
                 permute_w1(2)

@@ -28,6 +28,7 @@ UNITS = GROUPS * NEXP
 PAIR = 2
 PLANES = 2
 RUN = 8
+CHUNKS = WIDE // RUN
 TENSOR_COLS = 64
 GPSIMD_COLS = 64
 VECTOR_BANKS = {0: 2, 1: 1}
@@ -63,13 +64,10 @@ def tile_mspagent_pb_t_e_kernel(
         nc.vector.memset(w1_scales_raw[:].bitcast(I32), 0)
         nc.vector.memset(w2_scales[:].bitcast(I32), 0)
 
-        for first in range(0, GROUP, PAIR):
-            nc.sync.dma_start(out=h_sb[:, first : first + PAIR, :], in_=h_rows[:, first : first + PAIR, :])
-        for quadrant in range(4):
-            nc.sync.dma_start(
-                out=w1_scales_raw[32 * quadrant : 32 * quadrant + 16, :].bitcast(I32),
-                in_=e_w1_scales[:, 4 * quadrant : 4 * quadrant + 4, :].bitcast(I32),
-            )
+        def load_h_half(half):
+            tiles = slice(half * PAIR, (half + 1) * PAIR)
+            nc.sync.dma_start(out=h_sb[:, tiles, :], in_=h_rows[:, tiles, :])
+
         def load_w1(e):
             nc.sync.dma_start(out=w1_raw[:, e, :], in_=e_w1_words[e].rearrange("p n t -> p (n t)").bitcast(I32))
 
@@ -77,6 +75,13 @@ def tile_mspagent_pb_t_e_kernel(
             first = group * GROUP
             nc.sync.dma_start(out=h_sb[:, first : first + GROUP, :], in_=h_rows[:, first : first + GROUP, :])
 
+        load_h_half(0)
+        load_h_half(1)
+        for quadrant in range(4):
+            nc.sync.dma_start(
+                out=w1_scales_raw[32 * quadrant : 32 * quadrant + 16, :].bitcast(I32),
+                in_=e_w1_scales[:, 4 * quadrant : 4 * quadrant + 4, :].bitcast(I32),
+            )
         load_w1(0)
         load_w1(1)
         load_h(1)
@@ -132,32 +137,32 @@ def tile_mspagent_pb_t_e_kernel(
         zi_banks = {}
         x_banks, z_tiles, h1_grouped, h1_codes, h1_scales, y_banks, y_tiles, q_tiles = {}, {}, {}, {}, {}, {}, {}, {}
 
-        def transpose_h(group):
-            for half in range(GROUP // PAIR):
-                ht = psum_h.tile([P, PLANES, PAIR, P], F32, tag="ht")
-                for j in range(PAIR):
-                    words = h_sb[:, GROUP * group + PAIR * half + j, :].bitcast(F32)
-                    for u in range(PLANES):
-                        nc.tensor.transpose(ht[:, u, j, :], words[:, u : HID // 2 : PLANES], identity[:])
-                ht_banks[group, half] = ht
+        def transpose_h(group, half):
+            ht = psum_h.tile([P, PLANES, PAIR, P], F32, tag="ht")
+            for j in range(PAIR):
+                words = h_sb[:, GROUP * group + PAIR * half + j, :].bitcast(F32)
+                for u in range(PLANES):
+                    nc.tensor.transpose(ht[:, u, j, :], words[:, u : HID // 2 : PLANES], identity[:])
+            ht_banks[group, half] = ht
 
-        def regroup_h(group):
-            grouped = work.tile([P, GROUP, P, PACK], BF16, tag="h_grouped", align_bytes=64)
-            for half in range(GROUP // PAIR):
-                nc.scalar.copy(
-                    out=grouped[:, PAIR * half : PAIR * (half + 1)]
-                    .rearrange("p j m t -> p (j m t)")
-                    .bitcast(F32)
-                    .rearrange("p (q u) -> p q u", u=PLANES),
-                    in_=ht_banks[group, half][:].rearrange("p u j m -> p (j m) u"),
-                )
-            h_grouped[group] = grouped
+        def regroup_h(group, half):
+            if half == 0:
+                grouped_new = work.tile([P, GROUP, P, PACK], BF16, tag="h_grouped", align_bytes=64)
+                h_grouped[group] = grouped_new
+            nc.scalar.copy(
+                out=h_grouped[group][:, PAIR * half : PAIR * (half + 1)]
+                .rearrange("p j m t -> p (j m t)")
+                .bitcast(F32)
+                .rearrange("p (q u) -> p q u", u=PLANES),
+                in_=ht_banks[group, half][:].rearrange("p u j m -> p (j m) u"),
+            )
 
-        def quantise_h(group):
+        def quantise_h(group, tiles):
+            columns = slice(group * WIDE + tiles.start * P, group * WIDE + tiles.stop * P)
             nc.vector.quantize_mx(
-                out=h_codes[:, group * WIDE : (group + 1) * WIDE].bitcast(FP8X4),
-                scales=h_scales[:, group * WIDE : (group + 1) * WIDE],
-                in_=h_grouped[group][:].rearrange("p j m t -> p (j m t)"),
+                out=h_codes[:, columns].bitcast(FP8X4),
+                scales=h_scales[:, columns],
+                in_=h_grouped[group][:, tiles].rearrange("p j m t -> p (j m t)"),
             )
 
         def first_matmul(unit, t):
@@ -177,15 +182,17 @@ def tile_mspagent_pb_t_e_kernel(
         def relu(unit, t):
             e = unit % NEXP
             if t == 0:
-                z_new = work.tile([P, PACK, WIDE], BF16, tag="z")
+                z_new = work.tile([P, CHUNKS, PACK, RUN], BF16, tag="z", align_bytes=64)
                 z_tiles[unit] = z_new
             bias = b1[:, PACK * e + t : PACK * e + t + 1]
+            z_rows = z_tiles[unit][:, :, t, :]
+            x_rows = x_banks[unit, t][:].rearrange("p (c i) -> p c i", i=RUN)
             if t >= PACK - VECTOR_BANKS.get(unit, 0):
                 nc.vector.tensor_scalar(
-                    out=z_tiles[unit][:, t, :], in0=x_banks[unit, t][:], scalar1=bias, scalar2=0.0, op0=ADD, op1=MAX
+                    out=z_rows, in0=x_rows, scalar1=bias, scalar2=0.0, op0=ADD, op1=MAX
                 )
             else:
-                nc.scalar.activation(out=z_tiles[unit][:, t, :], in_=x_banks[unit, t][:], func=ACT.Relu, bias=bias)
+                nc.scalar.activation(out=z_rows, in_=x_rows, func=ACT.Relu, bias=bias)
 
         def interleave_vector(unit):
             grouped = work.tile([P, WIDE, PACK], BF16, tag="h1_grouped", align_bytes=64)
@@ -193,14 +200,14 @@ def tile_mspagent_pb_t_e_kernel(
             cut = WIDE - TENSOR_COLS - GPSIMD_COLS
             nc.vector.tensor_copy(
                 out=grouped[:, 0:cut, :].rearrange("p (c i) t -> p c t i", i=RUN),
-                in_=z_tiles[unit][:, :, 0:cut].rearrange("p t (c i) -> p c t i", i=RUN),
+                in_=z_tiles[unit][:, 0 : cut // RUN],
             )
 
         def interleave_gpsimd(unit):
             rows = slice(WIDE - TENSOR_COLS - GPSIMD_COLS - RUN, WIDE - TENSOR_COLS)
             nc.gpsimd.tensor_scalar(
-                out=h1_grouped[unit][:, rows, :],
-                in0=z_tiles[unit][:, :, rows].rearrange("p t c -> p c t"),
+                out=h1_grouped[unit][:, rows, :].rearrange("p (c i) t -> p c i t", i=RUN),
+                in0=z_tiles[unit][:, rows.start // RUN : rows.stop // RUN].rearrange("p c t i -> p c i t"),
                 scalar1=1.0,
                 scalar2=0.0,
                 op0=MULT,
@@ -212,7 +219,7 @@ def tile_mspagent_pb_t_e_kernel(
             nc.tensor.matmul(
                 out=zi[:].rearrange("p (c i) t -> p c t i", i=RUN),
                 lhsT=identity_bf16[:],
-                rhs=z_tiles[unit][:, :, WIDE - TENSOR_COLS : WIDE].rearrange("p t (c i) -> p c t i", i=RUN),
+                rhs=z_tiles[unit][:, (WIDE - TENSOR_COLS) // RUN : CHUNKS].rearrange("p c t i -> p (c t i)"),
                 start=True,
                 stop=True,
             )
@@ -282,12 +289,14 @@ def tile_mspagent_pb_t_e_kernel(
             if e == NEXP - 1:
                 nc.sync.dma_start(out=out_q[:, group * GROUP : (group + 1) * GROUP, :], in_=q[:])
 
-        transpose_h(0)
-        regroup_h(0)
+        for half in range(GROUP // PAIR):
+            transpose_h(0, half)
+            regroup_h(0, half)
+        quantise_h(0, slice(0, PAIR))
         permute_w1_scales()
         permute_w1(0)
-        nc.vector.tensor_copy(out=b1[:], in_=b1_raw[:].rearrange("p e t -> p (e t)"))
-        quantise_h(0)
+        quantise_h(0, slice(PAIR, GROUP))
+        nc.gpsimd.tensor_copy(out=b1[:], in_=b1_raw[:].rearrange("p e t -> p (e t)"))
         for t in range(PACK):
             first_matmul(0, t)
         permute_w1(1)
@@ -305,12 +314,20 @@ def tile_mspagent_pb_t_e_kernel(
             if 4 <= s:
                 gate(s - 4)
             if group + 1 < GROUPS and e == 2:
-                quantise_h(group + 1)
+                quantise_h(group + 1, slice(0, GROUP))
             for t in range(PACK):
                 if s < UNITS:
                     relu(s, t)
                 if s + 1 < UNITS:
                     first_matmul(s + 1, t)
+                if group + 1 < GROUPS:
+                    if e == 0 and t == 1:
+                        transpose_h(group + 1, 0)
+                        transpose_h(group + 1, 1)
+                    if e == 1 and t == 1:
+                        regroup_h(group + 1, 0)
+                    if e == 1 and t == PACK - 1:
+                        regroup_h(group + 1, 1)
                 if t == PACK - 1 and 1 <= s <= UNITS:
                     fetch_interleaved(s - 1)
                 if t == 2 and 2 <= s < UNITS + 2:
@@ -318,8 +335,3 @@ def tile_mspagent_pb_t_e_kernel(
             if s == 0:
                 permute_w1(2)
                 permute_w1(3)
-            if group + 1 < GROUPS:
-                if e == 0:
-                    transpose_h(group + 1)
-                if e == 1:
-                    regroup_h(group + 1)

@@ -93,15 +93,15 @@ def tile_mspagent_pb_t_e_kernel(
                 in_=e_w2_scales[:, 4 * quadrant : 4 * quadrant + 4, :].bitcast(I32),
             )
         nc.sync.dma_start(out=w2_words[:], in_=e_w2_words.rearrange("g p n t -> p g (n t)").bitcast(I32))
+        b2_all = keep.tile([P, NEXP * NACT], BF16)
+        nc.sync.dma_start(out=b2_all[:], in_=e_b2.rearrange("e a -> (e a)").partition_broadcast(P))
         for group in range(2, GROUPS):
             load_h(group)
 
         logits = keep.tile([P, TILES * NEXP], BF16)
         b1_raw = keep.tile([P, NEXP, PACK], BF16)
-        b2_all = keep.tile([P, NEXP * NACT], BF16)
         nc.scalar.dma_start(out=logits[:], in_=gate_logit.rearrange("(p i) e -> p (i e)", i=TILES))
         nc.scalar.dma_start(out=b1_raw[:], in_=e_b1.rearrange("e (p t) -> p e t", t=PACK))
-        nc.scalar.dma_start(out=b2_all[:], in_=e_b2.rearrange("e a -> (e a)").partition_broadcast(P))
 
         warm = keep.tile([P, 2], F32)
         nc.gpsimd.memset(warm[:], 0.0)

@@ -32,6 +32,8 @@ CHUNKS = WIDE // RUN
 TENSOR_COLS = 64
 GPSIMD_COLS = 64
 VECTOR_BANKS = {0: 2, 1: 1}
+IDLE_BEFORE = 2
+IDLE_BEHIND = 3
 
 FLOPS = 2 * ROWS * HID * HID * NEXP + 2 * ROWS * HID * NACT * NEXP
 
@@ -75,6 +77,9 @@ def tile_mspagent_pb_t_e_kernel(
             first = group * GROUP
             nc.sync.dma_start(out=h_sb[:, first : first + GROUP, :], in_=h_rows[:, first : first + GROUP, :])
 
+        idle_moving = keep.tile([P, WIDE], BF16)
+        nc.vector.memset(idle_moving[:], 0.0)
+
         load_h_half(0)
         load_h_half(1)
         for quadrant in range(4):
@@ -98,14 +103,13 @@ def tile_mspagent_pb_t_e_kernel(
         for group in range(2, GROUPS):
             load_h(group)
 
-        logits = keep.tile([P, TILES * NEXP], BF16)
-        b1_raw = keep.tile([P, NEXP, PACK], BF16)
-        nc.scalar.dma_start(out=logits[:], in_=gate_logit.rearrange("(p i) e -> p (i e)", i=TILES))
-        nc.scalar.dma_start(out=b1_raw[:], in_=e_b1.rearrange("e (p t) -> p e t", t=PACK))
-
         warm = keep.tile([P, 2], F32)
         nc.gpsimd.memset(warm[:], 0.0)
         nc.scalar.activation(out=warm[:, 1:2], in_=warm[:, 0:1], func=ACT.Sigmoid)
+        logits = keep.tile([P, TILES * NEXP], BF16)
+        b1_raw = keep.tile([P, NEXP, PACK], BF16)
+        nc.scalar.dma_start(out=b1_raw[:], in_=e_b1.rearrange("e (p t) -> p e t", t=PACK))
+        nc.scalar.dma_start(out=logits[:], in_=gate_logit.rearrange("(p i) e -> p (i e)", i=TILES))
 
         identity = keep.tile([P, P], F32)
         make_identity(nc, identity[:])
@@ -114,8 +118,12 @@ def tile_mspagent_pb_t_e_kernel(
 
         sigmoids = keep.tile([P, TILES * NEXP], F32)
         gates = keep.tile([P, TILES, NEXP], F32)
-        nc.scalar.activation(out=sigmoids[:], in_=logits[:], func=ACT.Sigmoid)
-        nc.gpsimd.tensor_scalar_mul(out=gates[:].rearrange("p i e -> p (i e)"), in0=sigmoids[:], scalar1=0.25)
+
+        def make_gates():
+            nc.scalar.activation(out=sigmoids[:], in_=logits[:], func=ACT.Sigmoid)
+            nc.gpsimd.tensor_scalar(
+                out=gates[:].rearrange("p i e -> p (i e)"), in0=sigmoids[:], scalar1=0.25, scalar2=0.0, op0=MULT, op1=ADD
+            )
 
         h_codes = keep.tile([P, TILES * P], U32, align_bytes=64)
         h_scales = keep.tile([P, TILES * P], U8, align_bytes=64)
@@ -243,7 +251,10 @@ def tile_mspagent_pb_t_e_kernel(
 
         def second_matmul(unit):
             e = unit % NEXP
-            y = psum_y.tile([P, GROUP, NACT], F32, tag="y")
+            if unit >= UNITS - NEXP and unit % 2 == 0:
+                y = psum_h.tile([P, GROUP, NACT], F32, tag="ht")
+            else:
+                y = psum_y.tile([P, GROUP, NACT], F32, tag="y")
             codes, scales = h1_codes[unit], h1_scales[unit]
             for j in range(GROUP):
                 nc.tensor.matmul_mx(
@@ -280,18 +291,29 @@ def tile_mspagent_pb_t_e_kernel(
             q = q_tiles[group]
             for j in range(GROUP):
                 factor = gates[:, group * GROUP + j, e : e + 1]
-                if e == 0:
+                if e == 0 and group == GROUPS - 1:
+                    nc.scalar.activation(out=q[:, j, :], in_=y_tiles[group][:, j, e, :], func=ACT.Copy, scale=factor)
+                elif e == 0:
                     nc.vector.tensor_scalar_mul(out=q[:, j, :], in0=y_tiles[group][:, j, e, :], scalar1=factor)
                 else:
                     nc.vector.scalar_tensor_tensor(
                         out=q[:, j, :], in0=y_tiles[group][:, j, e, :], scalar=factor, in1=q[:, j, :], op0=MULT, op1=ADD
                     )
-            if e == NEXP - 1:
+                if e == NEXP - 1 and group == GROUPS - 1:
+                    nc.sync.dma_start(out=out_q[:, group * GROUP + j, :], in_=q[:, j, :])
+            if e == NEXP - 1 and group < GROUPS - 1:
                 nc.sync.dma_start(out=out_q[:, group * GROUP : (group + 1) * GROUP, :], in_=q[:])
 
+        def keep_tensor_busy(count):
+            for i in range(count):
+                idle = psum_z.tile([P, WIDE], F32, tag="zi")
+                nc.tensor.matmul(out=idle[:], lhsT=idle_moving[:, 0:P], rhs=idle_moving[:], start=True, stop=True)
+
+        keep_tensor_busy(IDLE_BEFORE)
         for half in range(GROUP // PAIR):
             transpose_h(0, half)
             regroup_h(0, half)
+        keep_tensor_busy(IDLE_BEHIND)
         quantise_h(0, slice(0, PAIR))
         permute_w1_scales()
         permute_w1(0)
@@ -335,3 +357,4 @@ def tile_mspagent_pb_t_e_kernel(
             if s == 0:
                 permute_w1(2)
                 permute_w1(3)
+                make_gates()

@@ -29,7 +29,7 @@ PAIR = 2
 PLANES = 2
 RUN = 8
 CHUNKS = WIDE // RUN
-TENSOR_COLS = 64
+TENSOR_COLS = 80
 GPSIMD_COLS = 64
 VECTOR_BANKS = {0: 2, 1: 1}
 IDLE_BEFORE = 2

from contextlib import ExitStack

import concourse.mybir as mybir
from concourse.masks import make_identity

F32 = mybir.dt.float32
BF16 = mybir.dt.bfloat16
U8 = mybir.dt.uint8
U32 = mybir.dt.uint32
I32 = mybir.dt.int32
FP8X4 = mybir.dt.float8_e4m3fn_x4
ADD = mybir.AluOpType.add
MULT = mybir.AluOpType.mult
MAX = mybir.AluOpType.max
ACT = mybir.ActivationFunctionType

P = 128
ROWS = 4096
HID = 512
NEXP = 4
NACT = 128
PACK = 4
TILES = ROWS // P
GROUP = 4
GROUPS = TILES // GROUP
WIDE = GROUP * P
UNITS = GROUPS * NEXP
PAIR = 2
PLANES = 2
RUN = 8
CHUNKS = WIDE // RUN
TENSOR_COLS = 80
GPSIMD_COLS = 64
VECTOR_BANKS = {0: 2, 1: 1}
IDLE_BEFORE = 2
IDLE_BEHIND = 3

FLOPS = 2 * ROWS * HID * HID * NEXP + 2 * ROWS * HID * NACT * NEXP


def tile_mspagent_pb_t_e_kernel(
    tc, h, gate_logit, e_w1_words, e_w1_scales, e_b1, e_w2_words, e_w2_scales, e_b2, out_0, out_1
):
    nc = tc.nc
    with ExitStack() as ctx:
        keep = ctx.enter_context(tc.tile_pool(name="keep", bufs=1))
        work = ctx.enter_context(tc.tile_pool(name="work", bufs=4))
        outs = ctx.enter_context(tc.tile_pool(name="outs", bufs=3))
        psum_x = ctx.enter_context(tc.psum_pool(name="psum_x", bufs=4))
        psum_y = ctx.enter_context(tc.psum_pool(name="psum_y", bufs=1))
        psum_z = ctx.enter_context(tc.psum_pool(name="psum_z", bufs=1))
        psum_h = ctx.enter_context(tc.psum_pool(name="psum_h", bufs=2))
        ctx.enter_context(tc.manual_schedule())

        h_rows = h.rearrange("(p i) k -> p i k", i=TILES)
        out_q = out_0.rearrange("(p i) a -> p i a", i=TILES)
        out_y = out_1.rearrange("(p i) e a -> p i e a", i=TILES)

        h_sb = keep.tile([P, TILES, HID], BF16)
        w1_raw = keep.tile([P, NEXP, HID], I32, align_bytes=64)
        w1_words = keep.tile([P, NEXP, HID], I32, align_bytes=64)
        w2_words = keep.tile([P, NEXP, NACT], I32, align_bytes=64)
        w1_scales_raw = keep.tile([P, HID], U8, align_bytes=64)
        w1_scales = keep.tile([P, HID], U8, align_bytes=64)
        w2_scales = keep.tile([P, NACT], U8, align_bytes=64)
        nc.vector.memset(w1_scales_raw[:].bitcast(I32), 0)
        nc.vector.memset(w2_scales[:].bitcast(I32), 0)

        def load_h_half(half):
            tiles = slice(half * PAIR, (half + 1) * PAIR)
            nc.sync.dma_start(out=h_sb[:, tiles, :], in_=h_rows[:, tiles, :])

        def load_w1(e):
            nc.sync.dma_start(out=w1_raw[:, e, :], in_=e_w1_words[e].rearrange("p n t -> p (n t)").bitcast(I32))

        def load_h(group):
            first = group * GROUP
            nc.sync.dma_start(out=h_sb[:, first : first + GROUP, :], in_=h_rows[:, first : first + GROUP, :])

        idle_moving = keep.tile([P, WIDE], BF16)
        nc.vector.memset(idle_moving[:], 0.0)

        load_h_half(0)
        load_h_half(1)
        for quadrant in range(4):
            nc.sync.dma_start(
                out=w1_scales_raw[32 * quadrant : 32 * quadrant + 16, :].bitcast(I32),
                in_=e_w1_scales[:, 4 * quadrant : 4 * quadrant + 4, :].bitcast(I32),
            )
        load_w1(0)
        load_w1(1)
        load_h(1)
        load_w1(2)
        load_w1(3)
        for quadrant in range(4):
            nc.sync.dma_start(
                out=w2_scales[32 * quadrant : 32 * quadrant + 16, :].bitcast(I32),
                in_=e_w2_scales[:, 4 * quadrant : 4 * quadrant + 4, :].bitcast(I32),
            )
        nc.sync.dma_start(out=w2_words[:], in_=e_w2_words.rearrange("g p n t -> p g (n t)").bitcast(I32))
        b2_all = keep.tile([P, NEXP * NACT], BF16)
        nc.sync.dma_start(out=b2_all[:], in_=e_b2.rearrange("e a -> (e a)").partition_broadcast(P))
        for group in range(2, GROUPS):
            load_h(group)

        warm = keep.tile([P, 2], F32)
        nc.gpsimd.memset(warm[:], 0.0)
        nc.scalar.activation(out=warm[:, 1:2], in_=warm[:, 0:1], func=ACT.Sigmoid)
        logits = keep.tile([P, TILES * NEXP], BF16)
        b1_raw = keep.tile([P, NEXP, PACK], BF16)
        nc.scalar.dma_start(out=b1_raw[:], in_=e_b1.rearrange("e (p t) -> p e t", t=PACK))
        nc.scalar.dma_start(out=logits[:], in_=gate_logit.rearrange("(p i) e -> p (i e)", i=TILES))

        identity = keep.tile([P, P], F32)
        make_identity(nc, identity[:])
        identity_bf16 = keep.tile([P, P], BF16)
        make_identity(nc, identity_bf16[:])

        sigmoids = keep.tile([P, TILES * NEXP], F32)
        gates = keep.tile([P, TILES, NEXP], F32)

        def make_gates():
            nc.scalar.activation(out=sigmoids[:], in_=logits[:], func=ACT.Sigmoid)
            nc.gpsimd.tensor_scalar(
                out=gates[:].rearrange("p i e -> p (i e)"), in0=sigmoids[:], scalar1=0.25, scalar2=0.0, op0=MULT, op1=ADD
            )

        h_codes = keep.tile([P, TILES * P], U32, align_bytes=64)
        h_scales = keep.tile([P, TILES * P], U8, align_bytes=64)
        b1 = keep.tile([P, NEXP * PACK], F32)

        def permute_w1_scales():
            nc.vector.tensor_copy(
                out=w1_scales[:].rearrange("p (t m) -> p m t", t=PACK),
                in_=w1_scales_raw[:].rearrange("p (m t) -> p m t", t=PACK),
            )

        def permute_w1(e):
            nc.vector.tensor_copy(
                out=w1_words[:, e, :].rearrange("p (t m) -> p t m", t=PACK),
                in_=w1_raw[:, e, :].rearrange("p (m t) -> p t m", t=PACK),
            )

        ht_banks, h_grouped = {}, {}
        zi_banks = {}
        x_banks, z_tiles, h1_grouped, h1_codes, h1_scales, y_banks, y_tiles, q_tiles = {}, {}, {}, {}, {}, {}, {}, {}

        def transpose_h(group, half):
            ht = psum_h.tile([P, PLANES, PAIR, P], F32, tag="ht")
            for j in range(PAIR):
                words = h_sb[:, GROUP * group + PAIR * half + j, :].bitcast(F32)
                for u in range(PLANES):
                    nc.tensor.transpose(ht[:, u, j, :], words[:, u : HID // 2 : PLANES], identity[:])
            ht_banks[group, half] = ht

        def regroup_h(group, half):
            if half == 0:
                grouped_new = work.tile([P, GROUP, P, PACK], BF16, tag="h_grouped", align_bytes=64)
                h_grouped[group] = grouped_new
            nc.scalar.copy(
                out=h_grouped[group][:, PAIR * half : PAIR * (half + 1)]
                .rearrange("p j m t -> p (j m t)")
                .bitcast(F32)
                .rearrange("p (q u) -> p q u", u=PLANES),
                in_=ht_banks[group, half][:].rearrange("p u j m -> p (j m) u"),
            )

        def quantise_h(group, tiles):
            columns = slice(group * WIDE + tiles.start * P, group * WIDE + tiles.stop * P)
            nc.vector.quantize_mx(
                out=h_codes[:, columns].bitcast(FP8X4),
                scales=h_scales[:, columns],
                in_=h_grouped[group][:, tiles].rearrange("p j m t -> p (j m t)"),
            )

        def first_matmul(unit, t):
            group, e = divmod(unit, NEXP)
            x = psum_x.tile([P, WIDE], F32, tag="x")
            nc.tensor.matmul_mx(
                out=x[:],
                lhsT=w1_words[:, e, t * P : (t + 1) * P].bitcast(FP8X4),
                lhsT_scale=w1_scales[4 * e : P, t * P : (t + 1) * P],
                rhs=h_codes[:, group * WIDE : (group + 1) * WIDE].bitcast(FP8X4),
                rhs_scale=h_scales[:, group * WIDE : (group + 1) * WIDE],
                start=True,
                stop=True,
            )
            x_banks[unit, t] = x

        def relu(unit, t):
            e = unit % NEXP
            if t == 0:
                z_new = work.tile([P, CHUNKS, PACK, RUN], BF16, tag="z", align_bytes=64)
                z_tiles[unit] = z_new
            bias = b1[:, PACK * e + t : PACK * e + t + 1]
            z_rows = z_tiles[unit][:, :, t, :]
            x_rows = x_banks[unit, t][:].rearrange("p (c i) -> p c i", i=RUN)
            if t >= PACK - VECTOR_BANKS.get(unit, 0):
                nc.vector.tensor_scalar(
                    out=z_rows, in0=x_rows, scalar1=bias, scalar2=0.0, op0=ADD, op1=MAX
                )
            else:
                nc.scalar.activation(out=z_rows, in_=x_rows, func=ACT.Relu, bias=bias)

        def interleave_vector(unit):
            grouped = work.tile([P, WIDE, PACK], BF16, tag="h1_grouped", align_bytes=64)
            h1_grouped[unit] = grouped
            cut = WIDE - TENSOR_COLS - GPSIMD_COLS
            nc.vector.tensor_copy(
                out=grouped[:, 0:cut, :].rearrange("p (c i) t -> p c t i", i=RUN),
                in_=z_tiles[unit][:, 0 : cut // RUN],
            )

        def interleave_gpsimd(unit):
            rows = slice(WIDE - TENSOR_COLS - GPSIMD_COLS - RUN, WIDE - TENSOR_COLS)
            nc.gpsimd.tensor_scalar(
                out=h1_grouped[unit][:, rows, :].rearrange("p (c i) t -> p c i t", i=RUN),
                in0=z_tiles[unit][:, rows.start // RUN : rows.stop // RUN].rearrange("p c t i -> p c i t"),
                scalar1=1.0,
                scalar2=0.0,
                op0=MULT,
                op1=ADD,
            )

        def interleave_tensor(unit):
            zi = psum_z.tile([P, TENSOR_COLS, PACK], BF16, tag="zi")
            nc.tensor.matmul(
                out=zi[:].rearrange("p (c i) t -> p c t i", i=RUN),
                lhsT=identity_bf16[:],
                rhs=z_tiles[unit][:, (WIDE - TENSOR_COLS) // RUN : CHUNKS].rearrange("p c t i -> p (c t i)"),
                start=True,
                stop=True,
            )
            zi_banks[unit] = zi

        def fetch_interleaved(unit):
            nc.scalar.copy(
                out=h1_grouped[unit][:, WIDE - TENSOR_COLS : WIDE, :].rearrange("p c t -> p (c t)"),
                in_=zi_banks[unit][:].rearrange("p c t -> p (c t)"),
            )

        def quantise_h1(unit):
            codes = work.tile([P, WIDE], U32, tag="h1_codes", align_bytes=64)
            scales = work.tile([P, WIDE], U8, tag="h1_scales", align_bytes=64)
            nc.vector.quantize_mx(
                out=codes[:].bitcast(FP8X4),
                scales=scales[:],
                in_=h1_grouped[unit][:].rearrange("p c t -> p (c t)"),
            )
            h1_codes[unit], h1_scales[unit] = codes, scales

        def second_matmul(unit):
            e = unit % NEXP
            if unit >= UNITS - NEXP and unit % 2 == 0:
                y = psum_h.tile([P, GROUP, NACT], F32, tag="ht")
            else:
                y = psum_y.tile([P, GROUP, NACT], F32, tag="y")
            codes, scales = h1_codes[unit], h1_scales[unit]
            for j in range(GROUP):
                nc.tensor.matmul_mx(
                    out=y[:, j, :],
                    lhsT=codes[:, j * P : (j + 1) * P].bitcast(FP8X4),
                    lhsT_scale=scales[:, j * P : (j + 1) * P],
                    rhs=w2_words[:, e, :].bitcast(FP8X4),
                    rhs_scale=w2_scales[4 * e : P, :],
                    start=True,
                    stop=True,
                )
            y_banks[unit] = y

        def add_bias_2(unit):
            group, e = divmod(unit, NEXP)
            if e == 0:
                y_new = outs.tile([P, GROUP, NEXP, NACT], F32, tag="y_sb")
                y_tiles[group] = y_new
            nc.vector.tensor_tensor(
                out=y_tiles[group][:, :, e, :],
                in0=y_banks[unit][:],
                in1=b2_all[:, e * NACT : (e + 1) * NACT].unsqueeze(1).to_broadcast([P, GROUP, NACT]),
                op=ADD,
            )
            nc.sync.dma_start(
                out=out_y[:, group * GROUP : (group + 1) * GROUP, e, :], in_=y_tiles[group][:, :, e, :]
            )

        def gate(unit):
            group, e = divmod(unit, NEXP)
            if e == 0:
                q_new = outs.tile([P, GROUP, NACT], F32, tag="final_q")
                q_tiles[group] = q_new
            q = q_tiles[group]
            for j in range(GROUP):
                factor = gates[:, group * GROUP + j, e : e + 1]
                if e == 0 and group == GROUPS - 1:
                    nc.scalar.activation(out=q[:, j, :], in_=y_tiles[group][:, j, e, :], func=ACT.Copy, scale=factor)
                elif e == 0:
                    nc.vector.tensor_scalar_mul(out=q[:, j, :], in0=y_tiles[group][:, j, e, :], scalar1=factor)
                else:
                    nc.vector.scalar_tensor_tensor(
                        out=q[:, j, :], in0=y_tiles[group][:, j, e, :], scalar=factor, in1=q[:, j, :], op0=MULT, op1=ADD
                    )
                if e == NEXP - 1 and group == GROUPS - 1:
                    nc.sync.dma_start(out=out_q[:, group * GROUP + j, :], in_=q[:, j, :])
            if e == NEXP - 1 and group < GROUPS - 1:
                nc.sync.dma_start(out=out_q[:, group * GROUP : (group + 1) * GROUP, :], in_=q[:])

        def keep_tensor_busy(count):
            for i in range(count):
                idle = psum_z.tile([P, WIDE], F32, tag="zi")
                nc.tensor.matmul(out=idle[:], lhsT=idle_moving[:, 0:P], rhs=idle_moving[:], start=True, stop=True)

        keep_tensor_busy(IDLE_BEFORE)
        for half in range(GROUP // PAIR):
            transpose_h(0, half)
            regroup_h(0, half)
        keep_tensor_busy(IDLE_BEHIND)
        quantise_h(0, slice(0, PAIR))
        permute_w1_scales()
        permute_w1(0)
        quantise_h(0, slice(PAIR, GROUP))
        nc.gpsimd.tensor_copy(out=b1[:], in_=b1_raw[:].rearrange("p e t -> p (e t)"))
        for t in range(PACK):
            first_matmul(0, t)
        permute_w1(1)

        for s in range(UNITS + 4):
            group, e = divmod(s, NEXP)
            if 1 <= s <= UNITS:
                interleave_vector(s - 1)
                interleave_gpsimd(s - 1)
                interleave_tensor(s - 1)
            if 2 <= s < UNITS + 2:
                quantise_h1(s - 2)
            if 3 <= s < UNITS + 3:
                add_bias_2(s - 3)
            if 4 <= s:
                gate(s - 4)
            if group + 1 < GROUPS and e == 2:
                quantise_h(group + 1, slice(0, GROUP))
            for t in range(PACK):
                if s < UNITS:
                    relu(s, t)
                if s + 1 < UNITS:
                    first_matmul(s + 1, t)
                if group + 1 < GROUPS:
                    if e == 0 and t == 1:
                        transpose_h(group + 1, 0)
                        transpose_h(group + 1, 1)
                    if e == 1 and t == 1:
                        regroup_h(group + 1, 0)
                    if e == 1 and t == PACK - 1:
                        regroup_h(group + 1, 1)
                if t == PACK - 1 and 1 <= s <= UNITS:
                    fetch_interleaved(s - 1)
                if t == 2 and 2 <= s < UNITS + 2:
                    second_matmul(s - 2)
            if s == 0:
                permute_w1(2)
                permute_w1(3)
                make_gates()
